import numpy as np
import ml_dtypes


def mxq(x, axis, fmt="e4m3"):
    dtype, down = {"e4m3": (ml_dtypes.float8_e4m3fn, 7), "e5m2": (ml_dtypes.float8_e5m2, 14)}[fmt]
    v = np.moveaxis(np.asarray(x, np.float32).astype(ml_dtypes.bfloat16).astype(np.float64), axis, -1)
    blocks = v.reshape(v.shape[:-1] + (-1, 32))
    amax = np.abs(blocks).max(-1, keepdims=True)
    byte = np.maximum(np.where(amax > 0, np.frexp(amax)[1] - 1 + 127, 0) - down, 1)
    scale = np.exp2(byte - 127.0)
    codes = (blocks / scale).astype(np.float32).astype(dtype).astype(np.float64)
    return np.moveaxis((codes * scale).reshape(v.shape), -1, axis)


WIDE = False


def mx_kscale(k):
    if not WIDE:
        return np.ones(k)
    levels = np.array([10, -10, 5, -5, 0])
    a = np.random.permutation(np.resize(levels, k // 512 * 4)).reshape(k // 512, 4)
    idx = np.arange(k)
    return np.exp2(a[idx // 512, idx % 128 // 32])


BF16 = ml_dtypes.bfloat16


def bf(x):
    return np.asarray(x, np.float32).astype(BF16)


def f64(x):
    return np.asarray(x).astype(np.float64)


B, O, P, C, H, D, F = 24, 32, 223, 512, 4, 32, 4096
N = 1 + O + P
E = H * D
EPS = 1e-5


def layer_norm(t, g, b):
    m = t.mean(-1, keepdims=True)
    v = ((t - m) ** 2).mean(-1, keepdims=True)
    return (t - m) / np.sqrt(v + EPS) * g + b


def qkv_heads(t, w, b):
    y = (mxq(t, 2, "e4m3") @ mxq(w, 0, "e4m3")) + b
    y = y.reshape(t.shape[0], t.shape[1], 3, H, D)
    return [y[:, :, j].transpose(0, 2, 1, 3) for j in range(3)]


def mix(a, p):
    return np.concatenate([a[:, :, :1], p, a[:, :, 1:]], 2)


def setup_inputs():
    s = mx_kscale(C)
    r = np.random.standard_normal
    x = r((B, N, C)) * (0.5 + np.random.random((B, N, 1))) + 0.5 * r((B, N, 1))
    return {"x": bf(x),
            "w_qkv": bf(r((C, 3 * E)) / np.sqrt(C) / s[:, None]), "b_qkv": bf(0.2 * r(3 * E)),
            "w_qkv_p": bf(r((C, 3 * E)) / np.sqrt(C) / s[:, None]), "b_qkv_p": bf(0.2 * r(3 * E)),
            "n1_g": bf((1.0 + 0.1 * r(C)) * s), "n1_b": bf(0.2 * r(C) * s),
            "n1p_g": bf((1.0 + 0.1 * r(C)) * s), "n1p_b": bf(0.2 * r(C) * s)}


def reference(x, w_qkv, b_qkv, w_qkv_p, b_qkv_p, n1_g, n1_b, n1p_g, n1p_b):
    x = f64(x)
    pc = layer_norm(np.concatenate([x[:, :1], x[:, 1 + O:]], 1), f64(n1_g), f64(n1_b))
    pr = layer_norm(x[:, 1:1 + O], f64(n1p_g), f64(n1p_b))
    q_pc, k_pc, v_pc = qkv_heads(pc, f64(w_qkv), f64(b_qkv))
    q_pr, k_pr, v_pr = qkv_heads(pr, f64(w_qkv_p), f64(b_qkv_p))
    return mix(q_pc, q_pr), mix(k_pc, k_pr), mix(v_pc, v_pr)

@@ -1,0 +1,282 @@
+from contextlib import ExitStack
+
+import concourse.mybir as mybir
+from concourse.masks import make_identity
+
+BF16 = mybir.dt.bfloat16
+F32 = mybir.dt.float32
+U32 = mybir.dt.uint32
+U8 = mybir.dt.uint8
+FP8X4 = mybir.dt.float8_e4m3fn_x4
+ACT = mybir.ActivationFunctionType
+ALU = mybir.AluOpType
+
+P = 128
+PACK = 4
+SAMPLES = 24
+TOKENS = 256
+PROMPTS = 32
+CHANNELS = 512
+HEADS = 4
+HEAD_DIM = 32
+QKV = 3
+COLS = QKV * HEADS * HEAD_DIM
+QK_COLS = 256
+EPS = 1e-5
+
+PATCH_RUN = 7
+PATCH_ROWS = 32
+PATCH_SAMPLES = P // PATCH_ROWS
+PATCH_GROUPS = SAMPLES // PATCH_SAMPLES
+PROMPT_RUN = 8
+PROMPT_ROWS = PROMPTS // PROMPT_RUN
+PROMPT_PARTS = SAMPLES * PROMPT_ROWS
+
+FLOPS = 2 * SAMPLES * TOKENS * CHANNELS * COLS
+
+
+def tile_block_pa_t_kernel(
+    tc, x, w_qkv, b_qkv, w_qkv_p, b_qkv_p, n1_g, n1_b, n1p_g, n1p_b, out_0, out_1, out_2
+):
+    nc = tc.nc
+    outs = (out_0, out_1, out_2)
+    with ExitStack() as stack:
+        stack.enter_context(tc.manual_schedule())
+        const = stack.enter_context(tc.tile_pool(name="const", bufs=1))
+        resident = stack.enter_context(tc.tile_pool(name="resident", bufs=1))
+        stat = stack.enter_context(tc.tile_pool(name="stat", bufs=4))
+        zpool = stack.enter_context(tc.tile_pool(name="zpool", bufs=4))
+        work = stack.enter_context(tc.tile_pool(name="work", bufs=3))
+        ypool = stack.enter_context(tc.tile_pool(name="ypool", bufs=2))
+        psum_t = stack.enter_context(tc.psum_pool(name="psum_t", bufs=2))
+        psum_y = stack.enter_context(tc.psum_pool(name="psum_y", bufs=4))
+
+        eps_col = const.tile([P, 1], F32)
+        nc.vector.memset(eps_col[:], EPS)
+        table_warm = const.tile([P, 1], F32)
+        nc.scalar.activation(out=table_warm[:], in_=eps_col[:], func=ACT.Sqrt)
+        ident = const.tile([P, P], F32)
+        make_identity(nc, ident[:])
+        ones = const.tile([P, P], BF16)
+        nc.vector.memset(ones[:], 1.0)
+        bias_rows = const.tile([P, 2, COLS], BF16)
+        nc.vector.memset(bias_rows[:], 0.0)
+
+        w_raw = const.tile([P, 2, PACK, COLS], BF16)
+        for kind, w in enumerate((w_qkv, w_qkv_p)):
+            nc.sync.dma_start(
+                out=w_raw[:, kind, :, :], in_=w.rearrange("(p t) n -> p t n", t=PACK)
+            )
+        x_patch = []
+
+        def load_class_tokens(g):
+            nc.sync.dma_start(
+                out=x_patch[g][0:PATCH_SAMPLES, 0, :],
+                in_=x[g * PATCH_SAMPLES : (g + 1) * PATCH_SAMPLES, 0, :],
+            )
+
+        for g in range(PATCH_GROUPS):
+            xg = resident.tile([P, PATCH_RUN, CHANNELS], BF16, name="x_patch%d" % g)
+            x_patch.append(xg)
+            for s in range(PATCH_SAMPLES):
+                nc.sync.dma_start(
+                    out=xg[s:P:PATCH_SAMPLES, :, :],
+                    in_=x[g * PATCH_SAMPLES + s, PROMPTS:TOKENS, :].rearrange(
+                        "(m l) c -> m l c", l=PATCH_RUN
+                    ),
+                )
+            if g > 0:
+                load_class_tokens(g - 1)
+        load_class_tokens(PATCH_GROUPS - 1)
+        x_prompt = resident.tile([P, PROMPT_RUN, CHANNELS], BF16)
+        nc.vector.memset(x_prompt[PROMPT_PARTS:P, :, :], 0.0)
+        for m in range(PROMPT_ROWS):
+            nc.sync.dma_start(
+                out=x_prompt[m:PROMPT_PARTS:PROMPT_ROWS, :, :],
+                in_=x[:, 1 + m * PROMPT_RUN : 1 + (m + 1) * PROMPT_RUN, :],
+            )
+
+        norm_bf = const.tile([P, 4, 16], BF16)
+        for i, vec in enumerate((n1_g, n1_b, n1p_g, n1p_b)):
+            nc.scalar.dma_start(
+                out=norm_bf[:, i, 0:PACK], in_=vec.rearrange("(p t) -> p t", t=PACK)
+            )
+        for kind, bias in enumerate((b_qkv, b_qkv_p)):
+            nc.scalar.dma_start(out=bias_rows[0:1, kind, :], in_=bias.unsqueeze(0))
+        norm_col = const.tile([P, 4, PACK], F32)
+        nc.vector.tensor_copy(out=norm_col[:], in_=norm_bf[:, :, 0:PACK])
+        bias_all = const.tile([P, 2, COLS], F32)
+        for kind in range(2):
+            acc = psum_y.tile([P, COLS], F32)
+            nc.tensor.matmul(out=acc[:], lhsT=ones[:], rhs=bias_rows[:, kind, :], start=True, stop=True)
+            nc.vector.tensor_copy(out=bias_all[:, kind, :], in_=acc[:])
+
+        w_grouped = const.tile([P, 2, COLS, PACK], BF16, align_bytes=64)
+        w_codes = const.tile([P, 2, COLS], U32, align_bytes=64)
+        w_scales = const.tile([P, 2, COLS], U8, align_bytes=64)
+        for kind in range(2):
+            nc.scalar.copy(
+                out=w_grouped[:, kind, :, :], in_=w_raw[:, kind, :, :].rearrange("p t n -> p n t")
+            )
+
+        def quantise_weights():
+            for kind in range(2):
+                for lo, hi in ((0, QK_COLS), (QK_COLS, COLS)):
+                    nc.vector.quantize_mx(
+                        out=w_codes[:, kind, lo:hi].bitcast(FP8X4),
+                        scales=w_scales[:, kind, lo:hi],
+                        in_=w_grouped[:, kind, lo:hi, :].rearrange("p n t -> p (n t)"),
+                    )
+
+        def store_patch_group(g, y):
+            for s in range(PATCH_SAMPLES):
+                for j in range(QKV):
+                    nc.sync.dma_start(
+                        out=outs[j][g * PATCH_SAMPLES + s, :, PROMPTS:TOKENS, :].rearrange(
+                            "h (m l) d -> m h (l d)", l=PATCH_RUN
+                        ),
+                        in_=y[s:P:PATCH_SAMPLES, j * HEADS : (j + 1) * HEADS, :, :].rearrange(
+                            "p h l d -> p h (l d)"
+                        ),
+                    )
+            for j in range(QKV):
+                nc.sync.dma_start(
+                    out=outs[j][g * PATCH_SAMPLES : (g + 1) * PATCH_SAMPLES, :, 0, :],
+                    in_=y[0:PATCH_SAMPLES, j * HEADS : (j + 1) * HEADS, 0, :],
+                )
+
+        def store_prompt_group(g, y):
+            for m in range(PROMPT_ROWS):
+                for j in range(QKV):
+                    nc.sync.dma_start(
+                        out=outs[j][:, :, 1 + m * PROMPT_RUN : 1 + (m + 1) * PROMPT_RUN, :].rearrange(
+                            "b h l d -> b h (l d)"
+                        ),
+                        in_=y[m:PROMPT_PARTS:PROMPT_ROWS, j * HEADS : (j + 1) * HEADS, :, :].rearrange(
+                            "p h l d -> p h (l d)"
+                        ),
+                    )
+
+        tiles = []
+        for g in range(PATCH_GROUPS):
+            for slot in reversed(range(PATCH_RUN)):
+                tiles.append((0, x_patch[g], store_patch_group, g, PATCH_RUN, slot))
+        for slot in reversed(range(PROMPT_RUN)):
+            tiles.append((1, x_prompt, store_prompt_group, 0, PROMPT_RUN, slot))
+        pairs = len(tiles) // 2
+        live = {}
+
+        def statistics(i):
+            stats = stat.tile([P, 2, 6], F32)
+            mean_var = stat.tile([P, 2, 2], F32)
+            for s in range(2):
+                kind, xg, store, g, run, slot = tiles[2 * i + s]
+                nc.vector.bn_stats(out=stats[:, s, :], in_=xg[:, slot, :])
+                nc.vector.bn_aggr(out=mean_var[:, s, :], in_=stats[:, s, :])
+            live["mean_var", i] = mean_var
+
+        def inverse_std(i):
+            mean_var = live["mean_var", i]
+            std = stat.tile([P, 2], F32)
+            nc.scalar.activation(
+                out=std[:], in_=mean_var[:, :, 1], func=ACT.Sqrt, bias=eps_col[:, 0:1]
+            )
+            rstd = stat.tile([P, 2], F32)
+            nc.vector.reciprocal(out=rstd[:], in_=std[:])
+            neg_mean = stat.tile([P, 2], F32)
+            nc.gpsimd.tensor_scalar(
+                out=neg_mean[:], in0=mean_var[:, :, 0], scalar1=-1.0, scalar2=0.0,
+                op0=ALU.mult, op1=ALU.add,
+            )
+            live["rstd", i] = rstd
+            live["neg_mean", i] = neg_mean
+
+        def normalise_and_transpose(i):
+            rstd = live["rstd", i]
+            neg_mean = live["neg_mean", i]
+            banks = [psum_t.tile([P, 2, 2, P], F32, name="zT%d" % half) for half in range(2)]
+            for s in range(2):
+                kind, xg, store, g, run, slot = tiles[2 * i + s]
+                z = zpool.tile([P, PACK, P], F32)
+                nc.gpsimd.tensor_scalar(
+                    out=z[:],
+                    in0=xg[:, slot, :].rearrange("p (q t) -> p t q", t=PACK),
+                    scalar1=neg_mean[:, s : s + 1], scalar2=rstd[:, s : s + 1],
+                    op0=ALU.add, op1=ALU.mult,
+                )
+                for t in range(PACK):
+                    nc.tensor.transpose(banks[t // 2][:, t % 2, s, :], z[:, t, :], ident[:])
+            live["banks", i] = banks
+
+        def gain_shift_regroup(i):
+            banks = live["banks", i]
+            kind = tiles[2 * i][0]
+            planes = work.tile([P, PACK, 2 * P], BF16)
+            for t in range(PACK):
+                nc.scalar.activation(
+                    out=planes[:, t, :],
+                    in_=banks[t // 2][:, t % 2, :, :].rearrange("p s r -> p (s r)"),
+                    func=ACT.Identity,
+                    scale=norm_col[:, 2 * kind, t : t + 1], bias=norm_col[:, 2 * kind + 1, t : t + 1],
+                )
+            grouped = work.tile([P, 2 * P, PACK], BF16, align_bytes=64)
+            nc.scalar.copy(
+                out=grouped[:].rearrange("p (c i) t -> p c t i", i=4),
+                in_=planes[:].rearrange("p t (c i) -> p c t i", i=4),
+            )
+            live["grouped", i] = grouped
+
+        def quantise_and_multiply(i):
+            grouped = live["grouped", i]
+            kind = tiles[2 * i][0]
+            codes = work.tile([P, 2 * P], U32, align_bytes=64)
+            scales = work.tile([P, 2 * P], U8, align_bytes=64)
+            nc.vector.quantize_mx(
+                out=codes[:].bitcast(FP8X4), scales=scales[:],
+                in_=grouped[:].rearrange("p r t -> p (r t)"),
+            )
+            for s in range(2):
+                acc = psum_y.tile([P, COLS], F32)
+                for lo, hi in ((0, QK_COLS), (QK_COLS, COLS)):
+                    nc.tensor.matmul_mx(
+                        out=acc[:, lo:hi],
+                        lhsT=codes[:, s * P : (s + 1) * P].bitcast(FP8X4),
+                        lhsT_scale=scales[:, s * P : (s + 1) * P],
+                        rhs=w_codes[:, kind, lo:hi].bitcast(FP8X4),
+                        rhs_scale=w_scales[:, kind, lo:hi],
+                        start=True, stop=True,
+                    )
+                live["acc", i, s] = acc
+
+        def add_bias_and_store(i):
+            for s in range(2):
+                kind, xg, store, g, run, slot = tiles[2 * i + s]
+                acc = live["acc", i, s]
+                if slot == run - 1:
+                    y_new = ypool.tile([P, QKV * HEADS, run, HEAD_DIM], F32, name="y%d" % kind)
+                    live["y"] = y_new
+                y = live["y"]
+                nc.vector.tensor_tensor(
+                    out=y[:, :, slot, :],
+                    in0=acc[:].rearrange("p (a d) -> p a d", d=HEAD_DIM),
+                    in1=bias_all[:, kind, :].rearrange("p (a d) -> p a d", d=HEAD_DIM),
+                    op=ALU.add,
+                )
+                if slot == 0:
+                    store(g, y)
+
+        for n in range(-3, pairs + 1):
+            if 0 <= n - 1:
+                quantise_and_multiply(n - 1)
+            if 0 <= n + 2 < pairs:
+                inverse_std(n + 2)
+            if n + 3 < pairs:
+                statistics(n + 3)
+            if n == -1:
+                quantise_weights()
+            if 0 <= n + 1 < pairs:
+                normalise_and_transpose(n + 1)
+            if 0 <= n < pairs:
+                gain_shift_regroup(n)
+            if 0 <= n - 1:
+                add_bias_and_store(n - 1)

@@ -198,7 +198,7 @@ def tile_block_pa_t_kernel(
             for s in range(2):
                 kind, xg, store, g, run, slot = tiles[2 * i + s]
                 z = zpool.tile([P, PACK, P], F32)
-                nc.gpsimd.tensor_scalar(
+                nc.vector.tensor_scalar(
                     out=z[:],
                     in0=xg[:, slot, :].rearrange("p (q t) -> p t q", t=PACK),
                     scalar1=neg_mean[:, s : s + 1], scalar2=rstd[:, s : s + 1],

@@ -191,19 +191,24 @@ def tile_block_pa_t_kernel(
             live["rstd", i] = rstd
             live["neg_mean", i] = neg_mean
 
-        def normalise_and_transpose(i):
+        def normalise(i):
             rstd = live["rstd", i]
             neg_mean = live["neg_mean", i]
-            banks = [psum_t.tile([P, 2, 2, P], F32, name="zT%d" % half) for half in range(2)]
             for s in range(2):
                 kind, xg, store, g, run, slot = tiles[2 * i + s]
                 z = zpool.tile([P, PACK, P], F32)
-                nc.vector.tensor_scalar(
+                nc.gpsimd.tensor_scalar(
                     out=z[:],
                     in0=xg[:, slot, :].rearrange("p (q t) -> p t q", t=PACK),
                     scalar1=neg_mean[:, s : s + 1], scalar2=rstd[:, s : s + 1],
                     op0=ALU.add, op1=ALU.mult,
                 )
+                live["z", i, s] = z
+
+        def transpose(i):
+            banks = [psum_t.tile([P, 2, 2, P], F32, name="zT%d" % half) for half in range(2)]
+            for s in range(2):
+                z = live["z", i, s]
                 for t in range(PACK):
                     nc.tensor.transpose(banks[t // 2][:, t % 2, s, :], z[:, t, :], ident[:])
             live["banks", i] = banks
@@ -265,18 +270,20 @@ def tile_block_pa_t_kernel(
                 if slot == 0:
                     store(g, y)
 
-        for n in range(-3, pairs + 1):
-            if 0 <= n - 1:
-                quantise_and_multiply(n - 1)
+        for n in range(-4, pairs + 2):
             if 0 <= n + 2 < pairs:
-                inverse_std(n + 2)
-            if n + 3 < pairs:
-                statistics(n + 3)
+                normalise(n + 2)
+            if 0 <= n + 1 < pairs:
+                transpose(n + 1)
+            if 0 <= n - 1 < pairs:
+                quantise_and_multiply(n - 1)
+            if 0 <= n + 3 < pairs:
+                inverse_std(n + 3)
+            if n + 4 < pairs:
+                statistics(n + 4)
             if n == -1:
                 quantise_weights()
-            if 0 <= n + 1 < pairs:
-                normalise_and_transpose(n + 1)
             if 0 <= n < pairs:
                 gain_shift_regroup(n)
-            if 0 <= n - 1:
-                add_bias_and_store(n - 1)
+            if 0 <= n - 2:
+                add_bias_and_store(n - 2)

@@ -168,10 +168,15 @@ def tile_block_pa_t_kernel(
 
         def statistics(i):
             stats = stat.tile([P, 2, 6], F32)
-            mean_var = stat.tile([P, 2, 2], F32)
             for s in range(2):
                 kind, xg, store, g, run, slot = tiles[2 * i + s]
                 nc.vector.bn_stats(out=stats[:, s, :], in_=xg[:, slot, :])
+            live["stats", i] = stats
+
+        def mean_and_variance(i):
+            stats = live["stats", i]
+            mean_var = stat.tile([P, 2, 2], F32)
+            for s in range(2):
                 nc.vector.bn_aggr(out=mean_var[:, s, :], in_=stats[:, s, :])
             live["mean_var", i] = mean_var
 
@@ -213,7 +218,7 @@ def tile_block_pa_t_kernel(
                     nc.tensor.transpose(banks[t // 2][:, t % 2, s, :], z[:, t, :], ident[:])
             live["banks", i] = banks
 
-        def gain_shift_regroup(i):
+        def gain_and_shift(i):
             banks = live["banks", i]
             kind = tiles[2 * i][0]
             planes = work.tile([P, PACK, 2 * P], BF16)
@@ -224,6 +229,10 @@ def tile_block_pa_t_kernel(
                     func=ACT.Identity,
                     scale=norm_col[:, 2 * kind, t : t + 1], bias=norm_col[:, 2 * kind + 1, t : t + 1],
                 )
+            live["planes", i] = planes
+
+        def regroup(i):
+            planes = live["planes", i]
             grouped = work.tile([P, 2 * P, PACK], BF16, align_bytes=64)
             nc.scalar.copy(
                 out=grouped[:].rearrange("p (c i) t -> p c t i", i=4),
@@ -270,20 +279,24 @@ def tile_block_pa_t_kernel(
                 if slot == 0:
                     store(g, y)
 
-        for n in range(-4, pairs + 2):
+        for n in range(-4, pairs + 3):
             if 0 <= n + 2 < pairs:
                 normalise(n + 2)
             if 0 <= n + 1 < pairs:
                 transpose(n + 1)
-            if 0 <= n - 1 < pairs:
-                quantise_and_multiply(n - 1)
-            if 0 <= n + 3 < pairs:
-                inverse_std(n + 3)
+            if 0 <= n - 2 < pairs:
+                quantise_and_multiply(n - 2)
             if n + 4 < pairs:
                 statistics(n + 4)
+            if 0 <= n + 3 < pairs:
+                inverse_std(n + 3)
             if n == -1:
                 quantise_weights()
             if 0 <= n < pairs:
-                gain_shift_regroup(n)
-            if 0 <= n - 2:
-                add_bias_and_store(n - 2)
+                gain_and_shift(n)
+            if 0 <= n - 1 < pairs:
+                regroup(n - 1)
+            if 0 <= n - 3:
+                add_bias_and_store(n - 3)
+            if n + 4 < pairs:
+                mean_and_variance(n + 4)

@@ -180,21 +180,26 @@ def tile_block_pa_t_kernel(
                 nc.vector.bn_aggr(out=mean_var[:, s, :], in_=stats[:, s, :])
             live["mean_var", i] = mean_var
 
-        def inverse_std(i):
+        def standard_deviation(i):
             mean_var = live["mean_var", i]
             std = stat.tile([P, 2], F32)
             nc.scalar.activation(
                 out=std[:], in_=mean_var[:, :, 1], func=ACT.Sqrt, bias=eps_col[:, 0:1]
             )
-            rstd = stat.tile([P, 2], F32)
-            nc.vector.reciprocal(out=rstd[:], in_=std[:])
+            live["std", i] = std
+
+        def negate_mean(i):
             neg_mean = stat.tile([P, 2], F32)
             nc.gpsimd.tensor_scalar(
-                out=neg_mean[:], in0=mean_var[:, :, 0], scalar1=-1.0, scalar2=0.0,
+                out=neg_mean[:], in0=live["mean_var", i][:, :, 0], scalar1=-1.0, scalar2=0.0,
                 op0=ALU.mult, op1=ALU.add,
             )
-            live["rstd", i] = rstd
             live["neg_mean", i] = neg_mean
+
+        def invert(i):
+            rstd = stat.tile([P, 2], F32)
+            nc.vector.reciprocal(out=rstd[:], in_=live["std", i][:])
+            live["rstd", i] = rstd
 
         def normalise(i):
             rstd = live["rstd", i]
@@ -280,16 +285,18 @@ def tile_block_pa_t_kernel(
                     store(g, y)
 
         for n in range(-4, pairs + 3):
-            if 0 <= n + 2 < pairs:
-                normalise(n + 2)
             if 0 <= n + 1 < pairs:
                 transpose(n + 1)
             if 0 <= n - 2 < pairs:
                 quantise_and_multiply(n - 2)
+            if 0 <= n + 2 < pairs:
+                invert(n + 2)
+                normalise(n + 2)
             if n + 4 < pairs:
                 statistics(n + 4)
             if 0 <= n + 3 < pairs:
-                inverse_std(n + 3)
+                standard_deviation(n + 3)
+                negate_mean(n + 3)
             if n == -1:
                 quantise_weights()
             if 0 <= n < pairs:

@@ -31,6 +31,13 @@ PATCH_GROUPS = SAMPLES // PATCH_SAMPLES
 PROMPT_RUN = 8
 PROMPT_ROWS = PROMPTS // PROMPT_RUN
 PROMPT_PARTS = SAMPLES * PROMPT_ROWS
+SAMPLE_SPLIT = ((0, 16), (16, 24))
+
+UNIT = 4
+FIRST_UNIT = 2
+BATCH = 2
+STATS_LEAD = 6
+NORM_LEAD = 3
 
 FLOPS = 2 * SAMPLES * TOKENS * CHANNELS * COLS
 
@@ -44,11 +51,12 @@ def tile_block_pa_t_kernel(
         stack.enter_context(tc.manual_schedule())
         const = stack.enter_context(tc.tile_pool(name="const", bufs=1))
         resident = stack.enter_context(tc.tile_pool(name="resident", bufs=1))
-        stat = stack.enter_context(tc.tile_pool(name="stat", bufs=4))
-        zpool = stack.enter_context(tc.tile_pool(name="zpool", bufs=4))
-        work = stack.enter_context(tc.tile_pool(name="work", bufs=3))
-        ypool = stack.enter_context(tc.tile_pool(name="ypool", bufs=2))
-        psum_t = stack.enter_context(tc.psum_pool(name="psum_t", bufs=2))
+        stat = stack.enter_context(tc.tile_pool(name="stat", bufs=5))
+        zpool = stack.enter_context(tc.tile_pool(name="zpool", bufs=8))
+        work = stack.enter_context(tc.tile_pool(name="work", bufs=2))
+        unit_pool = stack.enter_context(tc.tile_pool(name="unit_pool", bufs=3))
+        ypool = stack.enter_context(tc.tile_pool(name="ypool", bufs=3))
+        psum_t = stack.enter_context(tc.psum_pool(name="psum_t", bufs=1))
         psum_y = stack.enter_context(tc.psum_pool(name="psum_y", bufs=4))
 
         eps_col = const.tile([P, 1], F32)
@@ -62,12 +70,22 @@ def tile_block_pa_t_kernel(
         bias_rows = const.tile([P, 2, COLS], BF16)
         nc.vector.memset(bias_rows[:], 0.0)
 
-        w_raw = const.tile([P, 2, PACK, COLS], BF16)
-        for kind, w in enumerate((w_qkv, w_qkv_p)):
-            nc.sync.dma_start(
-                out=w_raw[:, kind, :, :], in_=w.rearrange("(p t) n -> p t n", t=PACK)
-            )
         x_patch = []
+        for g in range(PATCH_GROUPS):
+            xg = resident.tile([P, PATCH_RUN, CHANNELS], BF16, name="x_patch%d" % g)
+            x_patch.append(xg)
+        x_prompt = resident.tile([P, PROMPT_RUN, CHANNELS], BF16)
+        nc.vector.memset(x_prompt[PROMPT_PARTS:P, :, :], 0.0)
+        w_raw = const.tile([P, 2, PACK, COLS], BF16)
+
+        def load_patch_slots(g, lo, hi):
+            for s in range(PATCH_SAMPLES):
+                nc.sync.dma_start(
+                    out=x_patch[g][s:P:PATCH_SAMPLES, lo:hi, :],
+                    in_=x[g * PATCH_SAMPLES + s, PROMPTS:TOKENS, :].rearrange(
+                        "(m l) c -> m l c", l=PATCH_RUN
+                    )[:, lo:hi, :],
+                )
 
         def load_class_tokens(g):
             nc.sync.dma_start(
@@ -75,26 +93,25 @@ def tile_block_pa_t_kernel(
                 in_=x[g * PATCH_SAMPLES : (g + 1) * PATCH_SAMPLES, 0, :],
             )
 
-        for g in range(PATCH_GROUPS):
-            xg = resident.tile([P, PATCH_RUN, CHANNELS], BF16, name="x_patch%d" % g)
-            x_patch.append(xg)
-            for s in range(PATCH_SAMPLES):
-                nc.sync.dma_start(
-                    out=xg[s:P:PATCH_SAMPLES, :, :],
-                    in_=x[g * PATCH_SAMPLES + s, PROMPTS:TOKENS, :].rearrange(
-                        "(m l) c -> m l c", l=PATCH_RUN
-                    ),
-                )
-            if g > 0:
-                load_class_tokens(g - 1)
-        load_class_tokens(PATCH_GROUPS - 1)
-        x_prompt = resident.tile([P, PROMPT_RUN, CHANNELS], BF16)
-        nc.vector.memset(x_prompt[PROMPT_PARTS:P, :, :], 0.0)
-        for m in range(PROMPT_ROWS):
+        def load_weights(kind, w):
             nc.sync.dma_start(
-                out=x_prompt[m:PROMPT_PARTS:PROMPT_ROWS, :, :],
-                in_=x[:, 1 + m * PROMPT_RUN : 1 + (m + 1) * PROMPT_RUN, :],
+                out=w_raw[:, kind, :, :], in_=w.rearrange("(p t) n -> p t n", t=PACK)
             )
+
+        load_patch_slots(0, PATCH_RUN - FIRST_UNIT, PATCH_RUN)
+        load_patch_slots(0, 0, PATCH_RUN - FIRST_UNIT)
+        load_weights(0, w_qkv)
+        for g in range(1, PATCH_GROUPS):
+            load_patch_slots(g, 0, PATCH_RUN)
+            load_class_tokens(g - 1)
+        load_class_tokens(PATCH_GROUPS - 1)
+        for m in range(PROMPT_ROWS):
+            for b0, b1 in SAMPLE_SPLIT:
+                nc.sync.dma_start(
+                    out=x_prompt[b0 * PROMPT_ROWS + m : b1 * PROMPT_ROWS : PROMPT_ROWS, :, :],
+                    in_=x[b0:b1, 1 + m * PROMPT_RUN : 1 + (m + 1) * PROMPT_RUN, :],
+                )
+        load_weights(1, w_qkv_p)
 
         norm_bf = const.tile([P, 4, 16], BF16)
         for i, vec in enumerate((n1_g, n1_b, n1p_g, n1p_b)):
@@ -104,31 +121,31 @@ def tile_block_pa_t_kernel(
         for kind, bias in enumerate((b_qkv, b_qkv_p)):
             nc.scalar.dma_start(out=bias_rows[0:1, kind, :], in_=bias.unsqueeze(0))
         norm_col = const.tile([P, 4, PACK], F32)
-        nc.vector.tensor_copy(out=norm_col[:], in_=norm_bf[:, :, 0:PACK])
+        nc.scalar.copy(out=norm_col[:], in_=norm_bf[:, :, 0:PACK])
         bias_all = const.tile([P, 2, COLS], F32)
         for kind in range(2):
             acc = psum_y.tile([P, COLS], F32)
             nc.tensor.matmul(out=acc[:], lhsT=ones[:], rhs=bias_rows[:, kind, :], start=True, stop=True)
-            nc.vector.tensor_copy(out=bias_all[:, kind, :], in_=acc[:])
+            nc.scalar.copy(out=bias_all[:, kind, :], in_=acc[:])
 
         w_grouped = const.tile([P, 2, COLS, PACK], BF16, align_bytes=64)
         w_codes = const.tile([P, 2, COLS], U32, align_bytes=64)
         w_scales = const.tile([P, 2, COLS], U8, align_bytes=64)
-        for kind in range(2):
+
+        def regroup_weights(kind):
             nc.scalar.copy(
                 out=w_grouped[:, kind, :, :], in_=w_raw[:, kind, :, :].rearrange("p t n -> p n t")
             )
 
-        def quantise_weights():
-            for kind in range(2):
-                for lo, hi in ((0, QK_COLS), (QK_COLS, COLS)):
-                    nc.vector.quantize_mx(
-                        out=w_codes[:, kind, lo:hi].bitcast(FP8X4),
-                        scales=w_scales[:, kind, lo:hi],
-                        in_=w_grouped[:, kind, lo:hi, :].rearrange("p n t -> p (n t)"),
-                    )
+        def quantise_weights(kind):
+            for lo, hi in ((0, QK_COLS), (QK_COLS, COLS)):
+                nc.vector.quantize_mx(
+                    out=w_codes[:, kind, lo:hi].bitcast(FP8X4),
+                    scales=w_scales[:, kind, lo:hi],
+                    in_=w_grouped[:, kind, lo:hi, :].rearrange("p n t -> p (n t)"),
+                )
 
-        def store_patch_group(g, y):
+        def store_patch_group(g, y, lo, hi):
             for s in range(PATCH_SAMPLES):
                 for j in range(QKV):
                     nc.sync.dma_start(
@@ -145,116 +162,158 @@ def tile_block_pa_t_kernel(
                     in_=y[0:PATCH_SAMPLES, j * HEADS : (j + 1) * HEADS, 0, :],
                 )
 
-        def store_prompt_group(g, y):
+        def store_prompt_group(g, y, lo, hi):
             for m in range(PROMPT_ROWS):
                 for j in range(QKV):
-                    nc.sync.dma_start(
-                        out=outs[j][:, :, 1 + m * PROMPT_RUN : 1 + (m + 1) * PROMPT_RUN, :].rearrange(
-                            "b h l d -> b h (l d)"
-                        ),
-                        in_=y[m:PROMPT_PARTS:PROMPT_ROWS, j * HEADS : (j + 1) * HEADS, :, :].rearrange(
-                            "p h l d -> p h (l d)"
-                        ),
-                    )
+                    for b0, b1 in SAMPLE_SPLIT:
+                        nc.sync.dma_start(
+                            out=outs[j][
+                                b0:b1, :, 1 + m * PROMPT_RUN + lo : 1 + m * PROMPT_RUN + hi, :
+                            ].rearrange("b h l d -> b h (l d)"),
+                            in_=y[
+                                b0 * PROMPT_ROWS + m : b1 * PROMPT_ROWS : PROMPT_ROWS,
+                                j * HEADS : (j + 1) * HEADS, lo:hi, :,
+                            ].rearrange("p h l d -> p h (l d)"),
+                        )
 
         tiles = []
         for g in range(PATCH_GROUPS):
             for slot in reversed(range(PATCH_RUN)):
-                tiles.append((0, x_patch[g], store_patch_group, g, PATCH_RUN, slot))
+                tiles.append(
+                    (0, x_patch[g], store_patch_group, g, PATCH_RUN, slot,
+                     (0, PATCH_RUN) if slot == 0 else None)
+                )
         for slot in reversed(range(PROMPT_RUN)):
-            tiles.append((1, x_prompt, store_prompt_group, 0, PROMPT_RUN, slot))
-        pairs = len(tiles) // 2
+            tiles.append(
+                (1, x_prompt, store_prompt_group, 0, PROMPT_RUN, slot,
+                 (slot, slot + UNIT) if slot % UNIT == 0 else None)
+            )
+        units = []
+        at = 0
+        while at < len(tiles):
+            size = FIRST_UNIT if at == 0 else UNIT
+            members = [i for i in range(at, min(at + size, len(tiles))) if tiles[i][0] == tiles[at][0]]
+            units.append(members)
+            at += len(members)
+        n_units = len(units)
         live = {}
 
-        def statistics(i):
-            stats = stat.tile([P, 2, 6], F32)
-            for s in range(2):
-                kind, xg, store, g, run, slot = tiles[2 * i + s]
-                nc.vector.bn_stats(out=stats[:, s, :], in_=xg[:, slot, :])
-            live["stats", i] = stats
+        batches = [[0], [1]] + [
+            list(range(u, min(u + BATCH, n_units))) for u in range(2, n_units, BATCH)
+        ]
+        place = {}
+        for k, members in enumerate(batches):
+            for r, u in enumerate(members):
+                place[u] = (k, r * UNIT)
+        WIDE = BATCH * UNIT
 
-        def mean_and_variance(i):
-            stats = live["stats", i]
-            mean_var = stat.tile([P, 2, 2], F32)
-            for s in range(2):
-                nc.vector.bn_aggr(out=mean_var[:, s, :], in_=stats[:, s, :])
-            live["mean_var", i] = mean_var
+        def statistics(u, part):
+            k, col = place[u]
+            if part == 0 and col == 0:
+                stats_new = stat.tile([P, WIDE, 6], F32, name="stats")
+                live["stats", k] = stats_new
+            stats = live["stats", k]
+            middle = len(units[u]) // 2
+            for s, i in enumerate(units[u]):
+                if (s >= middle) == (part == 1):
+                    kind, xg, store, g, run, slot, ready = tiles[i]
+                    nc.vector.bn_stats(out=stats[:, col + s, :], in_=xg[:, slot, :])
 
-        def standard_deviation(i):
-            mean_var = live["mean_var", i]
-            std = stat.tile([P, 2], F32)
-            nc.scalar.activation(
-                out=std[:], in_=mean_var[:, :, 1], func=ACT.Sqrt, bias=eps_col[:, 0:1]
-            )
-            live["std", i] = std
-
-        def negate_mean(i):
-            neg_mean = stat.tile([P, 2], F32)
+        def join_statistics(k):
+            n = place[batches[k][-1]][1] + len(units[batches[k][-1]])
+            stats = live["stats", k]
+            diff = stat.tile([P, WIDE], F32)
+            nc.gpsimd.tensor_tensor(out=diff[:, 0:n], in0=stats[:, 0:n, 1], in1=stats[:, 0:n, 4], op=ALU.subtract)
+            sums = stat.tile([P, WIDE, 2], F32)
+            nc.gpsimd.tensor_tensor(out=sums[:, 0:n, :], in0=stats[:, 0:n, 1:3], in1=stats[:, 0:n, 4:6], op=ALU.add)
+            square = stat.tile([P, WIDE], F32)
+            nc.gpsimd.tensor_tensor(out=square[:, 0:n], in0=diff[:, 0:n], in1=diff[:, 0:n], op=ALU.mult)
+            neg_mean = stat.tile([P, WIDE], F32)
             nc.gpsimd.tensor_scalar(
-                out=neg_mean[:], in0=live["mean_var", i][:, :, 0], scalar1=-1.0, scalar2=0.0,
+                out=neg_mean[:, 0:n], in0=sums[:, 0:n, 0], scalar1=-0.5, scalar2=0.0, op0=ALU.mult, op1=ALU.add
+            )
+            between = stat.tile([P, WIDE], F32)
+            nc.gpsimd.tensor_scalar(
+                out=between[:, 0:n], in0=square[:, 0:n], scalar1=CHANNELS / 4.0, scalar2=0.0,
                 op0=ALU.mult, op1=ALU.add,
             )
-            live["neg_mean", i] = neg_mean
+            spread = stat.tile([P, WIDE], F32)
+            nc.gpsimd.tensor_tensor(out=spread[:, 0:n], in0=between[:, 0:n], in1=sums[:, 0:n, 1], op=ALU.add)
+            std = stat.tile([P, WIDE], F32)
+            nc.scalar.activation(
+                out=std[:, 0:n], in_=spread[:, 0:n], func=ACT.Sqrt,
+                scale=1.0 / CHANNELS, bias=eps_col[:, 0:1],
+            )
+            live["neg_mean", k] = neg_mean
+            live["std", k] = std
 
-        def invert(i):
-            rstd = stat.tile([P, 2], F32)
-            nc.vector.reciprocal(out=rstd[:], in_=live["std", i][:])
-            live["rstd", i] = rstd
+        def invert(u):
+            k, col = place[u]
+            n = len(units[u])
+            rstd = stat.tile([P, UNIT], F32)
+            nc.vector.reciprocal(out=rstd[:, 0:n], in_=live["std", k][:, col : col + n])
+            live["rstd", u] = rstd
 
-        def normalise(i):
-            rstd = live["rstd", i]
-            neg_mean = live["neg_mean", i]
-            for s in range(2):
-                kind, xg, store, g, run, slot = tiles[2 * i + s]
+        def normalise(u):
+            rstd = live["rstd", u]
+            k, col = place[u]
+            neg_mean = live["neg_mean", k]
+            for s, i in enumerate(units[u]):
+                kind, xg, store, g, run, slot, ready = tiles[i]
                 z = zpool.tile([P, PACK, P], F32)
                 nc.gpsimd.tensor_scalar(
                     out=z[:],
                     in0=xg[:, slot, :].rearrange("p (q t) -> p t q", t=PACK),
-                    scalar1=neg_mean[:, s : s + 1], scalar2=rstd[:, s : s + 1],
+                    scalar1=neg_mean[:, col + s : col + s + 1], scalar2=rstd[:, s : s + 1],
                     op0=ALU.add, op1=ALU.mult,
                 )
-                live["z", i, s] = z
+                live["z", u, s] = z
 
-        def transpose(i):
-            banks = [psum_t.tile([P, 2, 2, P], F32, name="zT%d" % half) for half in range(2)]
-            for s in range(2):
-                z = live["z", i, s]
+        def transpose(u):
+            banks = [psum_t.tile([P, UNIT, P], F32, name="zT%d" % t) for t in range(PACK)]
+            for s in range(len(units[u])):
+                z = live["z", u, s]
                 for t in range(PACK):
-                    nc.tensor.transpose(banks[t // 2][:, t % 2, s, :], z[:, t, :], ident[:])
-            live["banks", i] = banks
+                    nc.tensor.transpose(banks[t][:, s, :], z[:, t, :], ident[:])
+            live["banks", u] = banks
 
-        def gain_and_shift(i):
-            banks = live["banks", i]
-            kind = tiles[2 * i][0]
-            planes = work.tile([P, PACK, 2 * P], BF16)
-            for t in range(PACK):
+        def gain_and_shift(u, first, last):
+            banks = live["banks", u]
+            n = len(units[u])
+            kind = tiles[units[u][0]][0]
+            if first == 0:
+                planes_new = work.tile([P, PACK, UNIT * P], BF16, name="planes")
+                live["planes", u] = planes_new
+            planes = live["planes", u]
+            for t in range(first, last):
                 nc.scalar.activation(
-                    out=planes[:, t, :],
-                    in_=banks[t // 2][:, t % 2, :, :].rearrange("p s r -> p (s r)"),
+                    out=planes[:, t, 0 : n * P],
+                    in_=banks[t][:, 0:n, :].rearrange("p s r -> p (s r)"),
                     func=ACT.Identity,
                     scale=norm_col[:, 2 * kind, t : t + 1], bias=norm_col[:, 2 * kind + 1, t : t + 1],
                 )
-            live["planes", i] = planes
 
-        def regroup(i):
-            planes = live["planes", i]
-            grouped = work.tile([P, 2 * P, PACK], BF16, align_bytes=64)
+        def regroup(u):
+            n = len(units[u])
+            planes = live["planes", u]
+            grouped = unit_pool.tile([P, UNIT * P, PACK], BF16, align_bytes=64)
             nc.scalar.copy(
-                out=grouped[:].rearrange("p (c i) t -> p c t i", i=4),
-                in_=planes[:].rearrange("p t (c i) -> p c t i", i=4),
+                out=grouped[:, 0 : n * P, :].rearrange("p (c i) t -> p c t i", i=4),
+                in_=planes[:, :, 0 : n * P].rearrange("p t (c i) -> p c t i", i=4),
             )
-            live["grouped", i] = grouped
+            live["grouped", u] = grouped
 
-        def quantise_and_multiply(i):
-            grouped = live["grouped", i]
-            kind = tiles[2 * i][0]
-            codes = work.tile([P, 2 * P], U32, align_bytes=64)
-            scales = work.tile([P, 2 * P], U8, align_bytes=64)
+        def quantise_and_multiply(u):
+            n = len(units[u])
+            grouped = live["grouped", u]
+            kind = tiles[units[u][0]][0]
+            codes = unit_pool.tile([P, UNIT * P], U32, align_bytes=64)
+            scales = unit_pool.tile([P, UNIT * P], U8, align_bytes=64)
             nc.vector.quantize_mx(
-                out=codes[:].bitcast(FP8X4), scales=scales[:],
-                in_=grouped[:].rearrange("p r t -> p (r t)"),
+                out=codes[:, 0 : n * P].bitcast(FP8X4), scales=scales[:, 0 : n * P],
+                in_=grouped[:, 0 : n * P, :].rearrange("p r t -> p (r t)"),
             )
-            for s in range(2):
+            for s in range(n):
                 acc = psum_y.tile([P, COLS], F32)
                 for lo, hi in ((0, QK_COLS), (QK_COLS, COLS)):
                     nc.tensor.matmul_mx(
@@ -265,12 +324,12 @@ def tile_block_pa_t_kernel(
                         rhs_scale=w_scales[:, kind, lo:hi],
                         start=True, stop=True,
                     )
-                live["acc", i, s] = acc
+                live["acc", u, s] = acc
 
-        def add_bias_and_store(i):
-            for s in range(2):
-                kind, xg, store, g, run, slot = tiles[2 * i + s]
-                acc = live["acc", i, s]
+        def add_bias_and_store(u):
+            for s, i in enumerate(units[u]):
+                kind, xg, store, g, run, slot, ready = tiles[i]
+                acc = live["acc", u, s]
                 if slot == run - 1:
                     y_new = ypool.tile([P, QKV * HEADS, run, HEAD_DIM], F32, name="y%d" % kind)
                     live["y"] = y_new
@@ -281,29 +340,45 @@ def tile_block_pa_t_kernel(
                     in1=bias_all[:, kind, :].rearrange("p (a d) -> p a d", d=HEAD_DIM),
                     op=ALU.add,
                 )
-                if slot == 0:
-                    store(g, y)
+                if ready is not None:
+                    store(g, y, ready[0], ready[1])
 
-        for n in range(-4, pairs + 3):
-            if 0 <= n + 1 < pairs:
-                transpose(n + 1)
-            if 0 <= n - 2 < pairs:
-                quantise_and_multiply(n - 2)
-            if 0 <= n + 2 < pairs:
-                invert(n + 2)
-                normalise(n + 2)
-            if n + 4 < pairs:
-                statistics(n + 4)
-            if 0 <= n + 3 < pairs:
-                standard_deviation(n + 3)
-                negate_mean(n + 3)
-            if n == -1:
-                quantise_weights()
-            if 0 <= n < pairs:
-                gain_and_shift(n)
-            if 0 <= n - 1 < pairs:
-                regroup(n - 1)
-            if 0 <= n - 3:
-                add_bias_and_store(n - 3)
-            if n + 4 < pairs:
-                mean_and_variance(n + 4)
+        first_prompt_unit = [u for u in range(n_units) if tiles[units[u][0]][0] == 1][0]
+        measured = []
+        joined = []
+        for c in range(-NORM_LEAD - 1, n_units):
+            if 0 <= c:
+                quantise_and_multiply(c)
+            last = min(2 * c + STATS_LEAD + 1, c + STATS_LEAD, n_units - 1) if c >= -NORM_LEAD else 0
+            fresh = list(range(len(measured), last + 1))
+            v = c + NORM_LEAD
+            for w in fresh[:1]:
+                statistics(w, 0)
+            if 0 <= v < n_units:
+                invert(v)
+                normalise(v)
+                transpose(v)
+                gain_and_shift(v, 0, 2)
+            for w in fresh[:1]:
+                statistics(w, 1)
+            for w in fresh[1:]:
+                statistics(w, 0)
+                statistics(w, 1)
+            measured.extend(fresh)
+            for k in range(len(batches)):
+                if k not in joined and batches[k][-1] in measured:
+                    join_statistics(k)
+                    joined.append(k)
+            if 0 <= v < n_units:
+                gain_and_shift(v, 2, PACK)
+                regroup(v)
+            if v == 0:
+                regroup_weights(0)
+            if c == -1:
+                quantise_weights(0)
+            if c == first_prompt_unit - 5:
+                regroup_weights(1)
+            if c == first_prompt_unit - 2:
+                quantise_weights(1)
+            if 0 <= c:
+                add_bias_and_store(c)

@@ -38,6 +38,9 @@ FIRST_UNIT = 2
 BATCH = 2
 STATS_LEAD = 6
 NORM_LEAD = 3
+EARLY_SLOTS = 3
+SPLIT_GROUPS = 0
+GPSIMD_UNITS = 0
 
 FLOPS = 2 * SAMPLES * TOKENS * CHANNELS * COLS
 
@@ -104,6 +107,8 @@ def tile_block_pa_t_kernel(
         for g in range(1, PATCH_GROUPS):
             load_patch_slots(g, 0, PATCH_RUN)
             load_class_tokens(g - 1)
+            if g == 2:
+                load_weights(1, w_qkv_p)
         load_class_tokens(PATCH_GROUPS - 1)
         for m in range(PROMPT_ROWS):
             for b0, b1 in SAMPLE_SPLIT:
@@ -111,7 +116,6 @@ def tile_block_pa_t_kernel(
                     out=x_prompt[b0 * PROMPT_ROWS + m : b1 * PROMPT_ROWS : PROMPT_ROWS, :, :],
                     in_=x[b0:b1, 1 + m * PROMPT_RUN : 1 + (m + 1) * PROMPT_RUN, :],
                 )
-        load_weights(1, w_qkv_p)
 
         norm_bf = const.tile([P, 4, 16], BF16)
         for i, vec in enumerate((n1_g, n1_b, n1p_g, n1p_b)):
@@ -150,17 +154,18 @@ def tile_block_pa_t_kernel(
                 for j in range(QKV):
                     nc.sync.dma_start(
                         out=outs[j][g * PATCH_SAMPLES + s, :, PROMPTS:TOKENS, :].rearrange(
-                            "h (m l) d -> m h (l d)", l=PATCH_RUN
-                        ),
-                        in_=y[s:P:PATCH_SAMPLES, j * HEADS : (j + 1) * HEADS, :, :].rearrange(
+                            "h (m l) d -> m h l d", l=PATCH_RUN
+                        )[:, :, lo:hi, :].rearrange("m h l d -> m h (l d)"),
+                        in_=y[s:P:PATCH_SAMPLES, j * HEADS : (j + 1) * HEADS, lo:hi, :].rearrange(
                             "p h l d -> p h (l d)"
                         ),
                     )
-            for j in range(QKV):
-                nc.sync.dma_start(
-                    out=outs[j][g * PATCH_SAMPLES : (g + 1) * PATCH_SAMPLES, :, 0, :],
-                    in_=y[0:PATCH_SAMPLES, j * HEADS : (j + 1) * HEADS, 0, :],
-                )
+            if lo == 0:
+                for j in range(QKV):
+                    nc.sync.dma_start(
+                        out=outs[j][g * PATCH_SAMPLES : (g + 1) * PATCH_SAMPLES, :, 0, :],
+                        in_=y[0:PATCH_SAMPLES, j * HEADS : (j + 1) * HEADS, 0, :],
+                    )
 
         def store_prompt_group(g, y, lo, hi):
             for m in range(PROMPT_ROWS):
@@ -177,17 +182,24 @@ def tile_block_pa_t_kernel(
                         )
 
         tiles = []
-        for g in range(PATCH_GROUPS):
-            for slot in reversed(range(PATCH_RUN)):
+
+        def patch_tiles(g, lo, hi):
+            for slot in reversed(range(lo, hi)):
                 tiles.append(
-                    (0, x_patch[g], store_patch_group, g, PATCH_RUN, slot,
-                     (0, PATCH_RUN) if slot == 0 else None)
+                    (0, x_patch[g], store_patch_group, g, PATCH_RUN, slot, (lo, hi) if slot == lo else None)
                 )
+
+        whole_groups = PATCH_GROUPS - SPLIT_GROUPS
+        for g in range(whole_groups):
+            patch_tiles(g, 0, PATCH_RUN)
+        for g in range(whole_groups, PATCH_GROUPS):
+            patch_tiles(g, 0, EARLY_SLOTS)
         for slot in reversed(range(PROMPT_RUN)):
             tiles.append(
-                (1, x_prompt, store_prompt_group, 0, PROMPT_RUN, slot,
-                 (slot, slot + UNIT) if slot % UNIT == 0 else None)
+                (1, x_prompt, store_prompt_group, 0, PROMPT_RUN, slot, (0, PROMPT_RUN) if slot == 0 else None)
             )
+        for g in range(whole_groups, PATCH_GROUPS):
+            patch_tiles(g, EARLY_SLOTS, PATCH_RUN)
         units = []
         at = 0
         while at < len(tiles):
@@ -293,15 +305,20 @@ def tile_block_pa_t_kernel(
                     scale=norm_col[:, 2 * kind, t : t + 1], bias=norm_col[:, 2 * kind + 1, t : t + 1],
                 )
 
-        def regroup(u):
+        def regroup(u, engine):
             n = len(units[u])
-            planes = live["planes", u]
-            grouped = unit_pool.tile([P, UNIT * P, PACK], BF16, align_bytes=64)
-            nc.scalar.copy(
-                out=grouped[:, 0 : n * P, :].rearrange("p (c i) t -> p c t i", i=4),
-                in_=planes[:, :, 0 : n * P].rearrange("p t (c i) -> p c t i", i=4),
-            )
-            live["grouped", u] = grouped
+            shared = u >= n_units - GPSIMD_UNITS
+            if engine == "scalar":
+                grouped_new = unit_pool.tile([P, UNIT * P, PACK], BF16, align_bytes=64, name="grouped")
+                live["grouped", u] = grouped_new
+            lo = n // 2 * P if engine == "gpsimd" else 0
+            hi = n // 2 * P if engine == "scalar" and shared else n * P
+            dst = live["grouped", u][:, lo:hi, :].rearrange("p (c i) t -> p c t i", i=4)
+            src = live["planes", u][:, :, lo:hi].rearrange("p t (c i) -> p c t i", i=4)
+            if engine == "scalar":
+                nc.scalar.copy(out=dst, in_=src)
+            elif shared:
+                nc.gpsimd.tensor_scalar(out=dst, in0=src, scalar1=1.0, scalar2=0.0, op0=ALU.mult, op1=ALU.add)
 
         def quantise_and_multiply(u):
             n = len(units[u])
@@ -330,10 +347,10 @@ def tile_block_pa_t_kernel(
             for s, i in enumerate(units[u]):
                 kind, xg, store, g, run, slot, ready = tiles[i]
                 acc = live["acc", u, s]
-                if slot == run - 1:
+                if ("y", kind, g) not in live:
                     y_new = ypool.tile([P, QKV * HEADS, run, HEAD_DIM], F32, name="y%d" % kind)
-                    live["y"] = y_new
-                y = live["y"]
+                    live["y", kind, g] = y_new
+                y = live["y", kind, g]
                 nc.vector.tensor_tensor(
                     out=y[:, :, slot, :],
                     in0=acc[:].rearrange("p (a d) -> p a d", d=HEAD_DIM),
@@ -359,6 +376,8 @@ def tile_block_pa_t_kernel(
                 normalise(v)
                 transpose(v)
                 gain_and_shift(v, 0, 2)
+            if 0 <= v - 1 < n_units:
+                regroup(v - 1, "gpsimd")
             for w in fresh[:1]:
                 statistics(w, 1)
             for w in fresh[1:]:
@@ -371,13 +390,11 @@ def tile_block_pa_t_kernel(
                     joined.append(k)
             if 0 <= v < n_units:
                 gain_and_shift(v, 2, PACK)
-                regroup(v)
-            if v == 0:
-                regroup_weights(0)
+                regroup(v, "scalar")
+            if 0 <= v <= 1:
+                regroup_weights(v)
             if c == -1:
                 quantise_weights(0)
-            if c == first_prompt_unit - 5:
-                regroup_weights(1)
             if c == first_prompt_unit - 2:
                 quantise_weights(1)
             if 0 <= c:

@@ -369,10 +369,13 @@ def tile_block_pa_t_kernel(
             last = min(2 * c + STATS_LEAD + 1, c + STATS_LEAD, n_units - 1) if c >= -NORM_LEAD else 0
             fresh = list(range(len(measured), last + 1))
             v = c + NORM_LEAD
+            if 0 <= c and v < n_units:
+                invert(v)
             for w in fresh[:1]:
                 statistics(w, 0)
             if 0 <= v < n_units:
-                invert(v)
+                if c < 0:
+                    invert(v)
                 normalise(v)
                 transpose(v)
                 gain_and_shift(v, 0, 2)

@@ -40,7 +40,7 @@ STATS_LEAD = 6
 NORM_LEAD = 3
 EARLY_SLOTS = 3
 SPLIT_GROUPS = 0
-GPSIMD_UNITS = 0
+GPSIMD_UNITS = 2
 
 FLOPS = 2 * SAMPLES * TOKENS * CHANNELS * COLS
 

from contextlib import ExitStack

import concourse.mybir as mybir
from concourse.masks import make_identity

BF16 = mybir.dt.bfloat16
F32 = mybir.dt.float32
U32 = mybir.dt.uint32
U8 = mybir.dt.uint8
FP8X4 = mybir.dt.float8_e4m3fn_x4
ACT = mybir.ActivationFunctionType
ALU = mybir.AluOpType

P = 128
PACK = 4
SAMPLES = 24
TOKENS = 256
PROMPTS = 32
CHANNELS = 512
HEADS = 4
HEAD_DIM = 32
QKV = 3
COLS = QKV * HEADS * HEAD_DIM
QK_COLS = 256
EPS = 1e-5

PATCH_RUN = 7
PATCH_ROWS = 32
PATCH_SAMPLES = P // PATCH_ROWS
PATCH_GROUPS = SAMPLES // PATCH_SAMPLES
PROMPT_RUN = 8
PROMPT_ROWS = PROMPTS // PROMPT_RUN
PROMPT_PARTS = SAMPLES * PROMPT_ROWS
SAMPLE_SPLIT = ((0, 16), (16, 24))

UNIT = 4
FIRST_UNIT = 2
BATCH = 2
STATS_LEAD = 6
NORM_LEAD = 3
EARLY_SLOTS = 3
SPLIT_GROUPS = 0
GPSIMD_UNITS = 2

FLOPS = 2 * SAMPLES * TOKENS * CHANNELS * COLS


def tile_block_pa_t_kernel(
    tc, x, w_qkv, b_qkv, w_qkv_p, b_qkv_p, n1_g, n1_b, n1p_g, n1p_b, out_0, out_1, out_2
):
    nc = tc.nc
    outs = (out_0, out_1, out_2)
    with ExitStack() as stack:
        stack.enter_context(tc.manual_schedule())
        const = stack.enter_context(tc.tile_pool(name="const", bufs=1))
        resident = stack.enter_context(tc.tile_pool(name="resident", bufs=1))
        stat = stack.enter_context(tc.tile_pool(name="stat", bufs=5))
        zpool = stack.enter_context(tc.tile_pool(name="zpool", bufs=8))
        work = stack.enter_context(tc.tile_pool(name="work", bufs=2))
        unit_pool = stack.enter_context(tc.tile_pool(name="unit_pool", bufs=3))
        ypool = stack.enter_context(tc.tile_pool(name="ypool", bufs=3))
        psum_t = stack.enter_context(tc.psum_pool(name="psum_t", bufs=1))
        psum_y = stack.enter_context(tc.psum_pool(name="psum_y", bufs=4))

        eps_col = const.tile([P, 1], F32)
        nc.vector.memset(eps_col[:], EPS)
        table_warm = const.tile([P, 1], F32)
        nc.scalar.activation(out=table_warm[:], in_=eps_col[:], func=ACT.Sqrt)
        ident = const.tile([P, P], F32)
        make_identity(nc, ident[:])
        ones = const.tile([P, P], BF16)
        nc.vector.memset(ones[:], 1.0)
        bias_rows = const.tile([P, 2, COLS], BF16)
        nc.vector.memset(bias_rows[:], 0.0)

        x_patch = []
        for g in range(PATCH_GROUPS):
            xg = resident.tile([P, PATCH_RUN, CHANNELS], BF16, name="x_patch%d" % g)
            x_patch.append(xg)
        x_prompt = resident.tile([P, PROMPT_RUN, CHANNELS], BF16)
        nc.vector.memset(x_prompt[PROMPT_PARTS:P, :, :], 0.0)
        w_raw = const.tile([P, 2, PACK, COLS], BF16)

        def load_patch_slots(g, lo, hi):
            for s in range(PATCH_SAMPLES):
                nc.sync.dma_start(
                    out=x_patch[g][s:P:PATCH_SAMPLES, lo:hi, :],
                    in_=x[g * PATCH_SAMPLES + s, PROMPTS:TOKENS, :].rearrange(
                        "(m l) c -> m l c", l=PATCH_RUN
                    )[:, lo:hi, :],
                )

        def load_class_tokens(g):
            nc.sync.dma_start(
                out=x_patch[g][0:PATCH_SAMPLES, 0, :],
                in_=x[g * PATCH_SAMPLES : (g + 1) * PATCH_SAMPLES, 0, :],
            )

        def load_weights(kind, w):
            nc.sync.dma_start(
                out=w_raw[:, kind, :, :], in_=w.rearrange("(p t) n -> p t n", t=PACK)
            )

        load_patch_slots(0, PATCH_RUN - FIRST_UNIT, PATCH_RUN)
        load_patch_slots(0, 0, PATCH_RUN - FIRST_UNIT)
        load_weights(0, w_qkv)
        for g in range(1, PATCH_GROUPS):
            load_patch_slots(g, 0, PATCH_RUN)
            load_class_tokens(g - 1)
            if g == 2:
                load_weights(1, w_qkv_p)
        load_class_tokens(PATCH_GROUPS - 1)
        for m in range(PROMPT_ROWS):
            for b0, b1 in SAMPLE_SPLIT:
                nc.sync.dma_start(
                    out=x_prompt[b0 * PROMPT_ROWS + m : b1 * PROMPT_ROWS : PROMPT_ROWS, :, :],
                    in_=x[b0:b1, 1 + m * PROMPT_RUN : 1 + (m + 1) * PROMPT_RUN, :],
                )

        norm_bf = const.tile([P, 4, 16], BF16)
        for i, vec in enumerate((n1_g, n1_b, n1p_g, n1p_b)):
            nc.scalar.dma_start(
                out=norm_bf[:, i, 0:PACK], in_=vec.rearrange("(p t) -> p t", t=PACK)
            )
        for kind, bias in enumerate((b_qkv, b_qkv_p)):
            nc.scalar.dma_start(out=bias_rows[0:1, kind, :], in_=bias.unsqueeze(0))
        norm_col = const.tile([P, 4, PACK], F32)
        nc.scalar.copy(out=norm_col[:], in_=norm_bf[:, :, 0:PACK])
        bias_all = const.tile([P, 2, COLS], F32)
        for kind in range(2):
            acc = psum_y.tile([P, COLS], F32)
            nc.tensor.matmul(out=acc[:], lhsT=ones[:], rhs=bias_rows[:, kind, :], start=True, stop=True)
            nc.scalar.copy(out=bias_all[:, kind, :], in_=acc[:])

        w_grouped = const.tile([P, 2, COLS, PACK], BF16, align_bytes=64)
        w_codes = const.tile([P, 2, COLS], U32, align_bytes=64)
        w_scales = const.tile([P, 2, COLS], U8, align_bytes=64)

        def regroup_weights(kind):
            nc.scalar.copy(
                out=w_grouped[:, kind, :, :], in_=w_raw[:, kind, :, :].rearrange("p t n -> p n t")
            )

        def quantise_weights(kind):
            for lo, hi in ((0, QK_COLS), (QK_COLS, COLS)):
                nc.vector.quantize_mx(
                    out=w_codes[:, kind, lo:hi].bitcast(FP8X4),
                    scales=w_scales[:, kind, lo:hi],
                    in_=w_grouped[:, kind, lo:hi, :].rearrange("p n t -> p (n t)"),
                )

        def store_patch_group(g, y, lo, hi):
            for s in range(PATCH_SAMPLES):
                for j in range(QKV):
                    nc.sync.dma_start(
                        out=outs[j][g * PATCH_SAMPLES + s, :, PROMPTS:TOKENS, :].rearrange(
                            "h (m l) d -> m h l d", l=PATCH_RUN
                        )[:, :, lo:hi, :].rearrange("m h l d -> m h (l d)"),
                        in_=y[s:P:PATCH_SAMPLES, j * HEADS : (j + 1) * HEADS, lo:hi, :].rearrange(
                            "p h l d -> p h (l d)"
                        ),
                    )
            if lo == 0:
                for j in range(QKV):
                    nc.sync.dma_start(
                        out=outs[j][g * PATCH_SAMPLES : (g + 1) * PATCH_SAMPLES, :, 0, :],
                        in_=y[0:PATCH_SAMPLES, j * HEADS : (j + 1) * HEADS, 0, :],
                    )

        def store_prompt_group(g, y, lo, hi):
            for m in range(PROMPT_ROWS):
                for j in range(QKV):
                    for b0, b1 in SAMPLE_SPLIT:
                        nc.sync.dma_start(
                            out=outs[j][
                                b0:b1, :, 1 + m * PROMPT_RUN + lo : 1 + m * PROMPT_RUN + hi, :
                            ].rearrange("b h l d -> b h (l d)"),
                            in_=y[
                                b0 * PROMPT_ROWS + m : b1 * PROMPT_ROWS : PROMPT_ROWS,
                                j * HEADS : (j + 1) * HEADS, lo:hi, :,
                            ].rearrange("p h l d -> p h (l d)"),
                        )

        tiles = []

        def patch_tiles(g, lo, hi):
            for slot in reversed(range(lo, hi)):
                tiles.append(
                    (0, x_patch[g], store_patch_group, g, PATCH_RUN, slot, (lo, hi) if slot == lo else None)
                )

        whole_groups = PATCH_GROUPS - SPLIT_GROUPS
        for g in range(whole_groups):
            patch_tiles(g, 0, PATCH_RUN)
        for g in range(whole_groups, PATCH_GROUPS):
            patch_tiles(g, 0, EARLY_SLOTS)
        for slot in reversed(range(PROMPT_RUN)):
            tiles.append(
                (1, x_prompt, store_prompt_group, 0, PROMPT_RUN, slot, (0, PROMPT_RUN) if slot == 0 else None)
            )
        for g in range(whole_groups, PATCH_GROUPS):
            patch_tiles(g, EARLY_SLOTS, PATCH_RUN)
        units = []
        at = 0
        while at < len(tiles):
            size = FIRST_UNIT if at == 0 else UNIT
            members = [i for i in range(at, min(at + size, len(tiles))) if tiles[i][0] == tiles[at][0]]
            units.append(members)
            at += len(members)
        n_units = len(units)
        live = {}

        batches = [[0], [1]] + [
            list(range(u, min(u + BATCH, n_units))) for u in range(2, n_units, BATCH)
        ]
        place = {}
        for k, members in enumerate(batches):
            for r, u in enumerate(members):
                place[u] = (k, r * UNIT)
        WIDE = BATCH * UNIT

        def statistics(u, part):
            k, col = place[u]
            if part == 0 and col == 0:
                stats_new = stat.tile([P, WIDE, 6], F32, name="stats")
                live["stats", k] = stats_new
            stats = live["stats", k]
            middle = len(units[u]) // 2
            for s, i in enumerate(units[u]):
                if (s >= middle) == (part == 1):
                    kind, xg, store, g, run, slot, ready = tiles[i]
                    nc.vector.bn_stats(out=stats[:, col + s, :], in_=xg[:, slot, :])

        def join_statistics(k):
            n = place[batches[k][-1]][1] + len(units[batches[k][-1]])
            stats = live["stats", k]
            diff = stat.tile([P, WIDE], F32)
            nc.gpsimd.tensor_tensor(out=diff[:, 0:n], in0=stats[:, 0:n, 1], in1=stats[:, 0:n, 4], op=ALU.subtract)
            sums = stat.tile([P, WIDE, 2], F32)
            nc.gpsimd.tensor_tensor(out=sums[:, 0:n, :], in0=stats[:, 0:n, 1:3], in1=stats[:, 0:n, 4:6], op=ALU.add)
            square = stat.tile([P, WIDE], F32)
            nc.gpsimd.tensor_tensor(out=square[:, 0:n], in0=diff[:, 0:n], in1=diff[:, 0:n], op=ALU.mult)
            neg_mean = stat.tile([P, WIDE], F32)
            nc.gpsimd.tensor_scalar(
                out=neg_mean[:, 0:n], in0=sums[:, 0:n, 0], scalar1=-0.5, scalar2=0.0, op0=ALU.mult, op1=ALU.add
            )
            between = stat.tile([P, WIDE], F32)
            nc.gpsimd.tensor_scalar(
                out=between[:, 0:n], in0=square[:, 0:n], scalar1=CHANNELS / 4.0, scalar2=0.0,
                op0=ALU.mult, op1=ALU.add,
            )
            spread = stat.tile([P, WIDE], F32)
            nc.gpsimd.tensor_tensor(out=spread[:, 0:n], in0=between[:, 0:n], in1=sums[:, 0:n, 1], op=ALU.add)
            std = stat.tile([P, WIDE], F32)
            nc.scalar.activation(
                out=std[:, 0:n], in_=spread[:, 0:n], func=ACT.Sqrt,
                scale=1.0 / CHANNELS, bias=eps_col[:, 0:1],
            )
            live["neg_mean", k] = neg_mean
            live["std", k] = std

        def invert(u):
            k, col = place[u]
            n = len(units[u])
            rstd = stat.tile([P, UNIT], F32)
            nc.vector.reciprocal(out=rstd[:, 0:n], in_=live["std", k][:, col : col + n])
            live["rstd", u] = rstd

        def normalise(u):
            rstd = live["rstd", u]
            k, col = place[u]
            neg_mean = live["neg_mean", k]
            for s, i in enumerate(units[u]):
                kind, xg, store, g, run, slot, ready = tiles[i]
                z = zpool.tile([P, PACK, P], F32)
                nc.gpsimd.tensor_scalar(
                    out=z[:],
                    in0=xg[:, slot, :].rearrange("p (q t) -> p t q", t=PACK),
                    scalar1=neg_mean[:, col + s : col + s + 1], scalar2=rstd[:, s : s + 1],
                    op0=ALU.add, op1=ALU.mult,
                )
                live["z", u, s] = z

        def transpose(u):
            banks = [psum_t.tile([P, UNIT, P], F32, name="zT%d" % t) for t in range(PACK)]
            for s in range(len(units[u])):
                z = live["z", u, s]
                for t in range(PACK):
                    nc.tensor.transpose(banks[t][:, s, :], z[:, t, :], ident[:])
            live["banks", u] = banks

        def gain_and_shift(u, first, last):
            banks = live["banks", u]
            n = len(units[u])
            kind = tiles[units[u][0]][0]
            if first == 0:
                planes_new = work.tile([P, PACK, UNIT * P], BF16, name="planes")
                live["planes", u] = planes_new
            planes = live["planes", u]
            for t in range(first, last):
                nc.scalar.activation(
                    out=planes[:, t, 0 : n * P],
                    in_=banks[t][:, 0:n, :].rearrange("p s r -> p (s r)"),
                    func=ACT.Identity,
                    scale=norm_col[:, 2 * kind, t : t + 1], bias=norm_col[:, 2 * kind + 1, t : t + 1],
                )

        def regroup(u, engine):
            n = len(units[u])
            shared = u >= n_units - GPSIMD_UNITS
            if engine == "scalar":
                grouped_new = unit_pool.tile([P, UNIT * P, PACK], BF16, align_bytes=64, name="grouped")
                live["grouped", u] = grouped_new
            lo = n // 2 * P if engine == "gpsimd" else 0
            hi = n // 2 * P if engine == "scalar" and shared else n * P
            dst = live["grouped", u][:, lo:hi, :].rearrange("p (c i) t -> p c t i", i=4)
            src = live["planes", u][:, :, lo:hi].rearrange("p t (c i) -> p c t i", i=4)
            if engine == "scalar":
                nc.scalar.copy(out=dst, in_=src)
            elif shared:
                nc.gpsimd.tensor_scalar(out=dst, in0=src, scalar1=1.0, scalar2=0.0, op0=ALU.mult, op1=ALU.add)

        def quantise_and_multiply(u):
            n = len(units[u])
            grouped = live["grouped", u]
            kind = tiles[units[u][0]][0]
            codes = unit_pool.tile([P, UNIT * P], U32, align_bytes=64)
            scales = unit_pool.tile([P, UNIT * P], U8, align_bytes=64)
            nc.vector.quantize_mx(
                out=codes[:, 0 : n * P].bitcast(FP8X4), scales=scales[:, 0 : n * P],
                in_=grouped[:, 0 : n * P, :].rearrange("p r t -> p (r t)"),
            )
            for s in range(n):
                acc = psum_y.tile([P, COLS], F32)
                for lo, hi in ((0, QK_COLS), (QK_COLS, COLS)):
                    nc.tensor.matmul_mx(
                        out=acc[:, lo:hi],
                        lhsT=codes[:, s * P : (s + 1) * P].bitcast(FP8X4),
                        lhsT_scale=scales[:, s * P : (s + 1) * P],
                        rhs=w_codes[:, kind, lo:hi].bitcast(FP8X4),
                        rhs_scale=w_scales[:, kind, lo:hi],
                        start=True, stop=True,
                    )
                live["acc", u, s] = acc

        def add_bias_and_store(u):
            for s, i in enumerate(units[u]):
                kind, xg, store, g, run, slot, ready = tiles[i]
                acc = live["acc", u, s]
                if ("y", kind, g) not in live:
                    y_new = ypool.tile([P, QKV * HEADS, run, HEAD_DIM], F32, name="y%d" % kind)
                    live["y", kind, g] = y_new
                y = live["y", kind, g]
                nc.vector.tensor_tensor(
                    out=y[:, :, slot, :],
                    in0=acc[:].rearrange("p (a d) -> p a d", d=HEAD_DIM),
                    in1=bias_all[:, kind, :].rearrange("p (a d) -> p a d", d=HEAD_DIM),
                    op=ALU.add,
                )
                if ready is not None:
                    store(g, y, ready[0], ready[1])

        first_prompt_unit = [u for u in range(n_units) if tiles[units[u][0]][0] == 1][0]
        measured = []
        joined = []
        for c in range(-NORM_LEAD - 1, n_units):
            if 0 <= c:
                quantise_and_multiply(c)
            last = min(2 * c + STATS_LEAD + 1, c + STATS_LEAD, n_units - 1) if c >= -NORM_LEAD else 0
            fresh = list(range(len(measured), last + 1))
            v = c + NORM_LEAD
            if 0 <= c and v < n_units:
                invert(v)
            for w in fresh[:1]:
                statistics(w, 0)
            if 0 <= v < n_units:
                if c < 0:
                    invert(v)
                normalise(v)
                transpose(v)
                gain_and_shift(v, 0, 2)
            if 0 <= v - 1 < n_units:
                regroup(v - 1, "gpsimd")
            for w in fresh[:1]:
                statistics(w, 1)
            for w in fresh[1:]:
                statistics(w, 0)
                statistics(w, 1)
            measured.extend(fresh)
            for k in range(len(batches)):
                if k not in joined and batches[k][-1] in measured:
                    join_statistics(k)
                    joined.append(k)
            if 0 <= v < n_units:
                gain_and_shift(v, 2, PACK)
                regroup(v, "scalar")
            if 0 <= v <= 1:
                regroup_weights(v)
            if c == -1:
                quantise_weights(0)
            if c == first_prompt_unit - 2:
                quantise_weights(1)
            if 0 <= c:
                add_bias_and_store(c)
